import numpy as np
import ml_dtypes


def mxq(x, axis, fmt="e4m3"):
    dtype, down = {"e4m3": (ml_dtypes.float8_e4m3fn, 7), "e5m2": (ml_dtypes.float8_e5m2, 14)}[fmt]
    v = np.moveaxis(np.asarray(x, np.float32).astype(ml_dtypes.bfloat16).astype(np.float64), axis, -1)
    blocks = v.reshape(v.shape[:-1] + (-1, 32))
    amax = np.abs(blocks).max(-1, keepdims=True)
    byte = np.maximum(np.where(amax > 0, np.frexp(amax)[1] - 1 + 127, 0) - down, 1)
    scale = np.exp2(byte - 127.0)
    codes = (blocks / scale).astype(np.float32).astype(dtype).astype(np.float64)
    return np.moveaxis((codes * scale).reshape(v.shape), -1, axis)


WIDE = False


def mx_kscale(k):
    if not WIDE:
        return np.ones(k)
    levels = np.array([10, -10, 5, -5, 0])
    a = np.random.permutation(np.resize(levels, k // 512 * 4)).reshape(k // 512, 4)
    idx = np.arange(k)
    return np.exp2(a[idx // 512, idx % 128 // 32])


BF16 = ml_dtypes.bfloat16


def bf(x):
    return np.asarray(x, np.float32).astype(BF16)


def f64(x):
    return np.asarray(x).astype(np.float64)


N, F, K, D, E = 256, 16384, 1536, 1024, 512
QS = 2.0
PS = 16.0


def setup_inputs():
    s, t = mx_kscale(F), mx_kscale(E)
    return {"x": bf(np.random.standard_normal((N, F)) * s),
            "Wy_w": bf(np.random.standard_normal((E, F)) * QS * F ** -0.5 / s[None, :] * t[:, None]),
            "Wy_b": bf(np.random.standard_normal(E) * 0.2 * t),
            "k": bf(np.random.standard_normal((K, E)) / t[None, :]),
            "prior": bf(np.random.uniform(size=K) * PS)}


def reference(x, Wy_w, Wy_b, k, prior):
    scale = 1.0 / (E ** 0.5)
    q = (mxq(f64(x), 1, "e4m3") @ mxq(f64(Wy_w), 1, "e4m3").T) + f64(Wy_b)
    sc = (mxq(q, 1, "e4m3") @ mxq(f64(k), 1, "e4m3").T) * scale
    e = np.exp(sc - sc.max(-1, keepdims=True))
    att = e / e.sum(-1, keepdims=True)
    return att * f64(prior)[None, :]

@@ -1,0 +1,267 @@
+from contextlib import ExitStack
+
+import concourse.mybir as mybir
+from concourse.masks import make_identity
+
+F32 = mybir.dt.float32
+BF16 = mybir.dt.bfloat16
+U32 = mybir.dt.uint32
+U8 = mybir.dt.uint8
+FP8X4 = mybir.dt.float8_e4m3fn_x4
+ACT = mybir.ActivationFunctionType
+ALU = mybir.AluOpType
+AXIS = mybir.AxisListType
+
+P = 128
+PASS = 4 * P
+PAIR = 2 * P
+BANK = 512
+
+ROWS, FEATURES, WIDTH, KEYS = 256, 16384, 512, 1536
+PASSES = FEATURES // PASS
+Q_TILES = WIDTH // P
+SCALE = WIDTH ** -0.5
+
+SLOT = 4 * PASS
+SLOTS = FEATURES // SLOT
+SLOT_PASSES = SLOT // PASS
+RAW_BUFS = 5
+STAGE_BUFS = 4
+RING = 4
+KEY_STEP = PASSES // 2
+KEY_PARTS = KEYS // BANK
+
+X_WORDS = PAIR
+W_WORDS = 2 * PAIR
+
+FLOPS = 2 * ROWS * FEATURES * WIDTH + 2 * ROWS * WIDTH * KEYS
+
+
+def piece_widths(slot):
+    if slot == 0:
+        return (PASS, PASS, 2 * PASS)
+    if slot == SLOTS - 1:
+        return (2 * PASS, PASS, PASS)
+    return (SLOT,)
+
+
+def tile_visualdeconfounder_pa_k_kernel(tc, x, Wy_w, Wy_b, k, prior, out):
+    nc = tc.nc
+    row_blocks = (x, Wy_w[0:PAIR, :], Wy_w[PAIR : 2 * PAIR, :])
+
+    with ExitStack() as ctx:
+        ctx.enter_context(tc.manual_schedule())
+        const = ctx.enter_context(tc.tile_pool(name="const", bufs=1))
+        raw_pool = ctx.enter_context(tc.tile_pool(name="raw", bufs=RAW_BUFS))
+        stage = ctx.enter_context(tc.tile_pool(name="stage", bufs=STAGE_BUFS))
+        small = ctx.enter_context(tc.tile_pool(name="small", bufs=2))
+
+        def load_slot(slot):
+            raw = raw_pool.tile([P, 2 * len(row_blocks), SLOT], BF16)
+            start = 0
+            for width in piece_widths(slot):
+                for b, rows in enumerate(row_blocks):
+                    nc.sync.dma_start(
+                        out=raw[:, 2 * b : 2 * b + 2, start : start + width],
+                        in_=rows[:, slot * SLOT + start : slot * SLOT + start + width].rearrange(
+                            "(p i) f -> p i f", i=2
+                        ),
+                    )
+                start += width
+            return raw
+
+        ident = const.tile([P, P], F32)
+        make_identity(nc, ident[:])
+        ones = const.tile([P, P], BF16)
+        nc.vector.memset(ones[:], 1.0)
+        prior_row = const.tile([P, KEYS], BF16)
+        nc.vector.memset(prior_row[:], 0.0)
+        nc.scalar.dma_start(out=prior_row[0:1, :], in_=prior.rearrange("(o j) -> o j", o=1))
+        bias_bf16 = const.tile([P, Q_TILES], BF16)
+        nc.scalar.dma_start(
+            out=bias_bf16[:].rearrange("p (u i) -> p u i", i=2),
+            in_=Wy_b.rearrange("(u p i) -> p u i", u=2, i=2),
+        )
+        bias = const.tile([P, Q_TILES], F32)
+        nc.gpsimd.tensor_copy(out=bias[:], in_=bias_bf16[:])
+        warm = const.tile([P, 1], F32)
+        nc.vector.memset(warm[:], 0.0)
+        nc.scalar.activation(out=warm[:], in_=warm[:], func=ACT.Exp)
+
+        raws = {}
+        keys_raw = const.tile([P, KEYS // P, WIDTH], BF16)
+        for slot in range(RAW_BUFS):
+            raws[slot] = load_slot(slot)
+            if slot == 2:
+                for part in range(KEY_PARTS):
+                    nc.sync.dma_start(
+                        out=keys_raw[:, 4 * part : 4 * part + 4, :],
+                        in_=k[BANK * part : BANK * (part + 1), :].rearrange("(j p) e -> p j e", p=P),
+                    )
+
+        key_codes = const.tile([P, KEYS], U32, align_bytes=64)
+        key_scales = const.tile([P, KEYS], U8, align_bytes=64)
+        q_codes = const.tile([P, ROWS], U32, align_bytes=64)
+        q_scales = const.tile([P, ROWS], U8, align_bytes=64)
+        prior_all = const.tile([P, KEYS], F32)
+
+        with tc.psum_pool(name="acc", bufs=1) as acc_pool, tc.psum_pool(name="ring", bufs=RING) as ring:
+            acc = [acc_pool.tile([P, ROWS], F32, name="acc%d" % t) for t in range(Q_TILES)]
+
+            def transpose_pair(tiles, first, col):
+                bank = ring.tile([P, 2, PAIR], F32)
+                for i in range(2):
+                    words = tiles[:, first + i, col : col + PASS].bitcast(F32)
+                    for u in range(2):
+                        nc.tensor.transpose(bank[:, u, i * P : (i + 1) * P], words[:, u * P : (u + 1) * P], ident[:])
+                return bank
+
+            def regroup(copy, grouped, first_word, bank):
+                halves = grouped[:].bitcast(F32)[:, 2 * first_word : 2 * (first_word + PAIR)]
+                copy(out=halves.rearrange("p (c u) -> p c u", u=2), in_=bank[:].rearrange("p u c -> p c u"))
+
+            def quantise(grouped, codes, scales, first_word, words):
+                nc.vector.quantize_mx(
+                    out=codes[:, first_word : first_word + words].bitcast(FP8X4),
+                    scales=scales[:, first_word : first_word + words],
+                    in_=grouped[:, 4 * first_word : 4 * (first_word + words)],
+                )
+
+            for part in range(KEY_PARTS):
+                bank = ring.tile([P, 2, PAIR], F32)
+                spread = bank[:].rearrange("p u c -> p (u c)")
+                cols = slice(part * BANK, (part + 1) * BANK)
+                nc.tensor.matmul(spread, lhsT=ones[:], rhs=prior_row[:, cols], start=True, stop=True)
+                nc.scalar.copy(out=prior_all[:, cols], in_=spread)
+
+            staged = {}
+            packed = {}
+            key_staged = {}
+
+            def stage_in(g):
+                raw = raws[g // SLOT_PASSES]
+                col = (g % SLOT_PASSES) * PASS
+                grouped = stage.tile([P, 4 * (X_WORDS + W_WORDS)], BF16, align_bytes=64)
+                for b in range(len(row_blocks)):
+                    bank = transpose_pair(raw, 2 * b, col)
+                    regroup(nc.vector.tensor_copy if b == 0 else nc.scalar.copy, grouped, b * PAIR, bank)
+                staged[g] = grouped
+
+            def quantise_pass(g):
+                codes = stage.tile([P, X_WORDS + W_WORDS], U32, align_bytes=64)
+                scales = stage.tile([P, X_WORDS + W_WORDS], U8, align_bytes=64)
+                quantise(staged[g], codes, scales, 0, X_WORDS)
+                quantise(staged[g], codes, scales, X_WORDS, W_WORDS)
+                packed[g] = (codes, scales)
+
+            def multiply_pass(g):
+                codes, scales = packed[g]
+                for t in range(Q_TILES):
+                    w_cols = slice(X_WORDS + t * P, X_WORDS + (t + 1) * P)
+                    nc.tensor.matmul_mx(
+                        out=acc[t][:],
+                        lhsT=codes[:, w_cols].bitcast(FP8X4),
+                        lhsT_scale=scales[:, w_cols],
+                        rhs=codes[:, 0:X_WORDS].bitcast(FP8X4),
+                        rhs_scale=scales[:, 0:X_WORDS],
+                        start=(g == 0),
+                        stop=(g == PASSES - 1),
+                    )
+
+            def stage_in_keys(part):
+                grouped = stage.tile([P, 4 * BANK], BF16, align_bytes=64)
+                for half in range(2):
+                    bank = transpose_pair(keys_raw, 4 * part + 2 * half, 0)
+                    regroup(nc.scalar.copy, grouped, half * PAIR, bank)
+                key_staged[part] = grouped
+
+            def quantise_keys(part):
+                nc.vector.quantize_mx(
+                    out=key_codes[:, part * BANK : (part + 1) * BANK].bitcast(FP8X4),
+                    scales=key_scales[:, part * BANK : (part + 1) * BANK],
+                    in_=key_staged[part][:],
+                )
+
+            for step in range(PASSES + 2):
+                if step < PASSES:
+                    stage_in(step)
+                    if step % SLOT_PASSES == SLOT_PASSES - 1 and step // SLOT_PASSES + RAW_BUFS < SLOTS:
+                        raws[step // SLOT_PASSES + RAW_BUFS] = load_slot(step // SLOT_PASSES + RAW_BUFS)
+                if KEY_STEP <= step < KEY_STEP + KEY_PARTS:
+                    stage_in_keys(step - KEY_STEP)
+                if 1 <= step <= PASSES:
+                    quantise_pass(step - 1)
+                if KEY_STEP < step <= KEY_STEP + KEY_PARTS:
+                    quantise_keys(step - KEY_STEP - 1)
+                if step >= 2:
+                    multiply_pass(step - 2)
+
+            q_planes = const.tile([P, Q_TILES, ROWS], BF16)
+            for t in range(Q_TILES):
+                if t % 2 == 0:
+                    nc.scalar.activation(out=q_planes[:, t, :], in_=acc[t][:], func=ACT.Identity, bias=bias[:, t : t + 1])
+                else:
+                    nc.vector.tensor_scalar(
+                        out=q_planes[:, t, :], in0=acc[t][:], scalar1=bias[:, t : t + 1], scalar2=None, op0=ALU.add
+                    )
+            q_grouped = const.tile([P, ROWS, Q_TILES], BF16, align_bytes=64)
+            nc.vector.tensor_copy(out=q_grouped[:], in_=q_planes[:].rearrange("p t c -> p c t"))
+            nc.vector.quantize_mx(
+                out=q_codes[:].bitcast(FP8X4), scales=q_scales[:], in_=q_grouped[:].rearrange("p c t -> p (c t)")
+            )
+
+        out_rows = out.rearrange("(p i) j -> p i j", i=2)
+        weights = const.tile([P, 2, KEYS], F32)
+        with tc.psum_pool(name="scores", bufs=2 * KEY_PARTS) as score_pool:
+            scores = {}
+            for i in range(2):
+                for part in range(KEY_PARTS):
+                    score = score_pool.tile([P, BANK], F32)
+                    nc.tensor.matmul_mx(
+                        out=score[:],
+                        lhsT=q_codes[:, i * P : (i + 1) * P].bitcast(FP8X4),
+                        lhsT_scale=q_scales[:, i * P : (i + 1) * P],
+                        rhs=key_codes[:, part * BANK : (part + 1) * BANK].bitcast(FP8X4),
+                        rhs_scale=key_scales[:, part * BANK : (part + 1) * BANK],
+                        start=True,
+                        stop=True,
+                    )
+                    scores[i, part] = score
+
+            sums = {}
+            for i in range(2):
+                part_max = small.tile([P, KEY_PARTS], F32)
+                for part in range(KEY_PARTS):
+                    nc.vector.tensor_reduce(out=part_max[:, part : part + 1], in_=scores[i, part][:], axis=AXIS.X, op=ALU.max)
+                row_max = small.tile([P, 1], F32)
+                nc.vector.tensor_reduce(out=row_max[:], in_=part_max[:], axis=AXIS.X, op=ALU.max)
+                shift = small.tile([P, 1], F32)
+                nc.vector.tensor_scalar(out=shift[:], in0=row_max[:], scalar1=-SCALE, scalar2=None, op0=ALU.mult)
+                part_sum = small.tile([P, KEY_PARTS], F32)
+                for part in range(KEY_PARTS):
+                    nc.scalar.activation(
+                        out=weights[:, i, part * BANK : (part + 1) * BANK],
+                        in_=scores[i, part][:],
+                        func=ACT.Exp,
+                        bias=shift[:],
+                        scale=SCALE,
+                        accum_out=part_sum[:, part : part + 1],
+                    )
+                sums[i] = part_sum
+
+            for i in range(2):
+                row_sum = small.tile([P, 1], F32)
+                nc.vector.tensor_reduce(out=row_sum[:], in_=sums[i][:], axis=AXIS.X, op=ALU.add)
+                inverse = small.tile([P, 1], F32)
+                nc.vector.reciprocal(out=inverse[:], in_=row_sum[:])
+                for part in range(KEY_PARTS):
+                    cols = slice(part * BANK, (part + 1) * BANK)
+                    nc.vector.scalar_tensor_tensor(
+                        out=weights[:, i, cols],
+                        in0=weights[:, i, cols],
+                        scalar=inverse[:],
+                        in1=prior_all[:, cols],
+                        op0=ALU.mult,
+                        op1=ALU.mult,
+                    )
+                    nc.sync.dma_start(out=out_rows[:, i, cols], in_=weights[:, i, cols])

@@ -26,8 +26,11 @@ SLOT = 4 * PASS
 SLOTS = FEATURES // SLOT
 SLOT_PASSES = SLOT // PASS
 RAW_BUFS = 5
+RUN = 4
+LAG = 2
 STAGE_BUFS = 4
-RING = 4
+PACKED_BUFS = RUN + LAG
+RING = 6
 KEY_STEP = PASSES // 2
 KEY_PARTS = KEYS // BANK
 
@@ -54,6 +57,7 @@ def tile_visualdeconfounder_pa_k_kernel(tc, x, Wy_w, Wy_b, k, prior, out):
         const = ctx.enter_context(tc.tile_pool(name="const", bufs=1))
         raw_pool = ctx.enter_context(tc.tile_pool(name="raw", bufs=RAW_BUFS))
         stage = ctx.enter_context(tc.tile_pool(name="stage", bufs=STAGE_BUFS))
+        packed_pool = ctx.enter_context(tc.tile_pool(name="packed", bufs=PACKED_BUFS))
         small = ctx.enter_context(tc.tile_pool(name="small", bufs=2))
 
         def load_slot(slot):
@@ -72,11 +76,6 @@ def tile_visualdeconfounder_pa_k_kernel(tc, x, Wy_w, Wy_b, k, prior, out):
 
         ident = const.tile([P, P], F32)
         make_identity(nc, ident[:])
-        ones = const.tile([P, P], BF16)
-        nc.vector.memset(ones[:], 1.0)
-        prior_row = const.tile([P, KEYS], BF16)
-        nc.vector.memset(prior_row[:], 0.0)
-        nc.scalar.dma_start(out=prior_row[0:1, :], in_=prior.rearrange("(o j) -> o j", o=1))
         bias_bf16 = const.tile([P, Q_TILES], BF16)
         nc.scalar.dma_start(
             out=bias_bf16[:].rearrange("p (u i) -> p u i", i=2),
@@ -103,10 +102,10 @@ def tile_visualdeconfounder_pa_k_kernel(tc, x, Wy_w, Wy_b, k, prior, out):
         key_scales = const.tile([P, KEYS], U8, align_bytes=64)
         q_codes = const.tile([P, ROWS], U32, align_bytes=64)
         q_scales = const.tile([P, ROWS], U8, align_bytes=64)
-        prior_all = const.tile([P, KEYS], F32)
+        prior_all = const.tile([P, KEYS], BF16)
 
         with tc.psum_pool(name="acc", bufs=1) as acc_pool, tc.psum_pool(name="ring", bufs=RING) as ring:
-            acc = [acc_pool.tile([P, ROWS], F32, name="acc%d" % t) for t in range(Q_TILES)]
+            acc = [acc_pool.tile([P, 2, ROWS], F32, name="acc%d" % u) for u in range(Q_TILES // 2)]
 
             def transpose_pair(tiles, first, col):
                 bank = ring.tile([P, 2, PAIR], F32)
@@ -127,13 +126,6 @@ def tile_visualdeconfounder_pa_k_kernel(tc, x, Wy_w, Wy_b, k, prior, out):
                     in_=grouped[:, 4 * first_word : 4 * (first_word + words)],
                 )
 
-            for part in range(KEY_PARTS):
-                bank = ring.tile([P, 2, PAIR], F32)
-                spread = bank[:].rearrange("p u c -> p (u c)")
-                cols = slice(part * BANK, (part + 1) * BANK)
-                nc.tensor.matmul(spread, lhsT=ones[:], rhs=prior_row[:, cols], start=True, stop=True)
-                nc.scalar.copy(out=prior_all[:, cols], in_=spread)
-
             staged = {}
             packed = {}
             key_staged = {}
@@ -148,8 +140,8 @@ def tile_visualdeconfounder_pa_k_kernel(tc, x, Wy_w, Wy_b, k, prior, out):
                 staged[g] = grouped
 
             def quantise_pass(g):
-                codes = stage.tile([P, X_WORDS + W_WORDS], U32, align_bytes=64)
-                scales = stage.tile([P, X_WORDS + W_WORDS], U8, align_bytes=64)
+                codes = packed_pool.tile([P, X_WORDS + W_WORDS], U32, align_bytes=64)
+                scales = packed_pool.tile([P, X_WORDS + W_WORDS], U8, align_bytes=64)
                 quantise(staged[g], codes, scales, 0, X_WORDS)
                 quantise(staged[g], codes, scales, X_WORDS, W_WORDS)
                 packed[g] = (codes, scales)
@@ -159,13 +151,13 @@ def tile_visualdeconfounder_pa_k_kernel(tc, x, Wy_w, Wy_b, k, prior, out):
                 for t in range(Q_TILES):
                     w_cols = slice(X_WORDS + t * P, X_WORDS + (t + 1) * P)
                     nc.tensor.matmul_mx(
-                        out=acc[t][:],
+                        out=acc[t // 2][:, t % 2, :],
                         lhsT=codes[:, w_cols].bitcast(FP8X4),
                         lhsT_scale=scales[:, w_cols],
                         rhs=codes[:, 0:X_WORDS].bitcast(FP8X4),
                         rhs_scale=scales[:, 0:X_WORDS],
-                        start=(g == 0),
-                        stop=(g == PASSES - 1),
+                        start=(g == 0 and t % 2 == 0),
+                        stop=(g == PASSES - 1 and t % 2 == 1),
                     )
 
             def stage_in_keys(part):
@@ -182,27 +174,39 @@ def tile_visualdeconfounder_pa_k_kernel(tc, x, Wy_w, Wy_b, k, prior, out):
                     in_=key_staged[part][:],
                 )
 
-            for step in range(PASSES + 2):
-                if step < PASSES:
-                    stage_in(step)
-                    if step % SLOT_PASSES == SLOT_PASSES - 1 and step // SLOT_PASSES + RAW_BUFS < SLOTS:
-                        raws[step // SLOT_PASSES + RAW_BUFS] = load_slot(step // SLOT_PASSES + RAW_BUFS)
-                if KEY_STEP <= step < KEY_STEP + KEY_PARTS:
-                    stage_in_keys(step - KEY_STEP)
-                if 1 <= step <= PASSES:
-                    quantise_pass(step - 1)
-                if KEY_STEP < step <= KEY_STEP + KEY_PARTS:
-                    quantise_keys(step - KEY_STEP - 1)
-                if step >= 2:
-                    multiply_pass(step - 2)
+            for first in range(0, PASSES, RUN):
+                for g in range(first, first + RUN):
+                    stage_in(g)
+                    next_slot = g // SLOT_PASSES + RAW_BUFS
+                    if g % SLOT_PASSES == SLOT_PASSES - 1 and next_slot < SLOTS:
+                        raws[next_slot] = load_slot(next_slot)
+                        if next_slot == SLOTS - 1:
+                            nc.sync.dma_start(out=prior_all[:], in_=prior.partition_broadcast(P))
+                    if KEY_STEP <= g < KEY_STEP + KEY_PARTS:
+                        stage_in_keys(g - KEY_STEP)
+                    if g >= 1:
+                        quantise_pass(g - 1)
+                    if KEY_STEP < g <= KEY_STEP + KEY_PARTS:
+                        quantise_keys(g - KEY_STEP - 1)
+                for g in range(max(first - LAG, 0), first + RUN - LAG):
+                    multiply_pass(g)
+            quantise_pass(PASSES - 1)
+            for g in range(PASSES - LAG, PASSES):
+                multiply_pass(g)
 
             q_planes = const.tile([P, Q_TILES, ROWS], BF16)
             for t in range(Q_TILES):
-                if t % 2 == 0:
-                    nc.scalar.activation(out=q_planes[:, t, :], in_=acc[t][:], func=ACT.Identity, bias=bias[:, t : t + 1])
+                if t // 2 == 0:
+                    nc.scalar.activation(
+                        out=q_planes[:, t, :], in_=acc[t // 2][:, t % 2, :], func=ACT.Identity, bias=bias[:, t : t + 1]
+                    )
                 else:
                     nc.vector.tensor_scalar(
-                        out=q_planes[:, t, :], in0=acc[t][:], scalar1=bias[:, t : t + 1], scalar2=None, op0=ALU.add
+                        out=q_planes[:, t, :],
+                        in0=acc[t // 2][:, t % 2, :],
+                        scalar1=bias[:, t : t + 1],
+                        scalar2=None,
+                        op0=ALU.add,
                     )
             q_grouped = const.tile([P, ROWS, Q_TILES], BF16, align_bytes=64)
             nc.vector.tensor_copy(out=q_grouped[:], in_=q_planes[:].rearrange("p t c -> p c t"))

@@ -26,12 +26,11 @@ SLOT = 4 * PASS
 SLOTS = FEATURES // SLOT
 SLOT_PASSES = SLOT // PASS
 RAW_BUFS = 5
-RUN = 4
+RUN = 2
 LAG = 2
 STAGE_BUFS = 4
 PACKED_BUFS = RUN + LAG
 RING = 6
-KEY_STEP = PASSES // 2
 KEY_PARTS = KEYS // BANK
 
 X_WORDS = PAIR
@@ -74,6 +73,14 @@ def tile_visualdeconfounder_pa_k_kernel(tc, x, Wy_w, Wy_b, k, prior, out):
                 start += width
             return raw
 
+        def load_keys_and_prior():
+            for part in range(KEY_PARTS):
+                nc.sync.dma_start(
+                    out=keys_raw[:, 4 * part : 4 * part + 4, :],
+                    in_=k[BANK * part : BANK * (part + 1), :].rearrange("(j p) e -> p j e", p=P),
+                )
+            nc.sync.dma_start(out=prior_all[:], in_=prior.partition_broadcast(P))
+
         ident = const.tile([P, P], F32)
         make_identity(nc, ident[:])
         bias_bf16 = const.tile([P, Q_TILES], BF16)
@@ -91,12 +98,6 @@ def tile_visualdeconfounder_pa_k_kernel(tc, x, Wy_w, Wy_b, k, prior, out):
         keys_raw = const.tile([P, KEYS // P, WIDTH], BF16)
         for slot in range(RAW_BUFS):
             raws[slot] = load_slot(slot)
-            if slot == 2:
-                for part in range(KEY_PARTS):
-                    nc.sync.dma_start(
-                        out=keys_raw[:, 4 * part : 4 * part + 4, :],
-                        in_=k[BANK * part : BANK * (part + 1), :].rearrange("(j p) e -> p j e", p=P),
-                    )
 
         key_codes = const.tile([P, KEYS], U32, align_bytes=64)
         key_scales = const.tile([P, KEYS], U8, align_bytes=64)
@@ -164,7 +165,7 @@ def tile_visualdeconfounder_pa_k_kernel(tc, x, Wy_w, Wy_b, k, prior, out):
                 grouped = stage.tile([P, 4 * BANK], BF16, align_bytes=64)
                 for half in range(2):
                     bank = transpose_pair(keys_raw, 4 * part + 2 * half, 0)
-                    regroup(nc.scalar.copy, grouped, half * PAIR, bank)
+                    regroup(nc.scalar.copy if part % 2 == 0 else nc.vector.tensor_copy, grouped, half * PAIR, bank)
                 key_staged[part] = grouped
 
             def quantise_keys(part):
@@ -181,16 +182,15 @@ def tile_visualdeconfounder_pa_k_kernel(tc, x, Wy_w, Wy_b, k, prior, out):
                     if g % SLOT_PASSES == SLOT_PASSES - 1 and next_slot < SLOTS:
                         raws[next_slot] = load_slot(next_slot)
                         if next_slot == SLOTS - 1:
-                            nc.sync.dma_start(out=prior_all[:], in_=prior.partition_broadcast(P))
-                    if KEY_STEP <= g < KEY_STEP + KEY_PARTS:
-                        stage_in_keys(g - KEY_STEP)
+                            load_keys_and_prior()
                     if g >= 1:
                         quantise_pass(g - 1)
-                    if KEY_STEP < g <= KEY_STEP + KEY_PARTS:
-                        quantise_keys(g - KEY_STEP - 1)
                 for g in range(max(first - LAG, 0), first + RUN - LAG):
                     multiply_pass(g)
+
             quantise_pass(PASSES - 1)
+            stage_in_keys(0)
+            stage_in_keys(1)
             for g in range(PASSES - LAG, PASSES):
                 multiply_pass(g)
 
@@ -208,18 +208,21 @@ def tile_visualdeconfounder_pa_k_kernel(tc, x, Wy_w, Wy_b, k, prior, out):
                         scalar2=None,
                         op0=ALU.add,
                     )
+            stage_in_keys(2)
             q_grouped = const.tile([P, ROWS, Q_TILES], BF16, align_bytes=64)
             nc.vector.tensor_copy(out=q_grouped[:], in_=q_planes[:].rearrange("p t c -> p c t"))
             nc.vector.quantize_mx(
                 out=q_codes[:].bitcast(FP8X4), scales=q_scales[:], in_=q_grouped[:].rearrange("p c t -> p (c t)")
             )
+            for part in range(KEY_PARTS):
+                quantise_keys(part)
 
         out_rows = out.rearrange("(p i) j -> p i j", i=2)
         weights = const.tile([P, 2, KEYS], F32)
         with tc.psum_pool(name="scores", bufs=2 * KEY_PARTS) as score_pool:
             scores = {}
-            for i in range(2):
-                for part in range(KEY_PARTS):
+            for part in range(KEY_PARTS):
+                for i in range(2):
                     score = score_pool.tile([P, BANK], F32)
                     nc.tensor.matmul_mx(
                         out=score[:],

@@ -27,7 +27,7 @@ SLOTS = FEATURES // SLOT
 SLOT_PASSES = SLOT // PASS
 RAW_BUFS = 5
 RUN = 2
-LAG = 2
+LAG = 3
 STAGE_BUFS = 4
 PACKED_BUFS = RUN + LAG
 RING = 6
@@ -137,7 +137,7 @@ def tile_visualdeconfounder_pa_k_kernel(tc, x, Wy_w, Wy_b, k, prior, out):
                 grouped = stage.tile([P, 4 * (X_WORDS + W_WORDS)], BF16, align_bytes=64)
                 for b in range(len(row_blocks)):
                     bank = transpose_pair(raw, 2 * b, col)
-                    regroup(nc.vector.tensor_copy if b == 0 else nc.scalar.copy, grouped, b * PAIR, bank)
+                    regroup(nc.vector.tensor_copy if b == 0 and g % 2 == 0 else nc.scalar.copy, grouped, b * PAIR, bank)
                 staged[g] = grouped
 
             def quantise_pass(g):
@@ -189,9 +189,11 @@ def tile_visualdeconfounder_pa_k_kernel(tc, x, Wy_w, Wy_b, k, prior, out):
                     multiply_pass(g)
 
             quantise_pass(PASSES - 1)
+            for g in range(PASSES - LAG, PASSES - 2):
+                multiply_pass(g)
             stage_in_keys(0)
             stage_in_keys(1)
-            for g in range(PASSES - LAG, PASSES):
+            for g in range(PASSES - 2, PASSES):
                 multiply_pass(g)
 
             q_planes = const.tile([P, Q_TILES, ROWS], BF16)

@@ -25,11 +25,10 @@ SCALE = WIDTH ** -0.5
 SLOT = 4 * PASS
 SLOTS = FEATURES // SLOT
 SLOT_PASSES = SLOT // PASS
-RAW_BUFS = 5
-RUN = 2
-LAG = 3
-STAGE_BUFS = 4
-PACKED_BUFS = RUN + LAG
+RAW_BUFS = 4
+LAG = 2
+STAGE_BUFS = 2 * SLOT_PASSES
+PACKED_BUFS = 2 * SLOT_PASSES
 RING = 6
 KEY_PARTS = KEYS // BANK
 
@@ -73,7 +72,12 @@ def tile_visualdeconfounder_pa_k_kernel(tc, x, Wy_w, Wy_b, k, prior, out):
                 start += width
             return raw
 
-        def load_keys_and_prior():
+        def load_the_rest():
+            nc.sync.dma_start(
+                out=bias_bf16[:].rearrange("p (u i) -> p u i", i=2),
+                in_=Wy_b.rearrange("(u p i) -> p u i", u=2, i=2),
+            )
+            nc.gpsimd.tensor_copy(out=bias[:], in_=bias_bf16[:])
             for part in range(KEY_PARTS):
                 nc.sync.dma_start(
                     out=keys_raw[:, 4 * part : 4 * part + 4, :],
@@ -84,12 +88,7 @@ def tile_visualdeconfounder_pa_k_kernel(tc, x, Wy_w, Wy_b, k, prior, out):
         ident = const.tile([P, P], F32)
         make_identity(nc, ident[:])
         bias_bf16 = const.tile([P, Q_TILES], BF16)
-        nc.scalar.dma_start(
-            out=bias_bf16[:].rearrange("p (u i) -> p u i", i=2),
-            in_=Wy_b.rearrange("(u p i) -> p u i", u=2, i=2),
-        )
         bias = const.tile([P, Q_TILES], F32)
-        nc.gpsimd.tensor_copy(out=bias[:], in_=bias_bf16[:])
         warm = const.tile([P, 1], F32)
         nc.vector.memset(warm[:], 0.0)
         nc.scalar.activation(out=warm[:], in_=warm[:], func=ACT.Exp)
@@ -131,21 +130,22 @@ def tile_visualdeconfounder_pa_k_kernel(tc, x, Wy_w, Wy_b, k, prior, out):
             packed = {}
             key_staged = {}
 
-            def stage_in(g):
-                raw = raws[g // SLOT_PASSES]
-                col = (g % SLOT_PASSES) * PASS
-                grouped = stage.tile([P, 4 * (X_WORDS + W_WORDS)], BF16, align_bytes=64)
+            def stage_in(run):
+                for g in run:
+                    staged[g] = stage.tile([P, 4 * (X_WORDS + W_WORDS)], BF16, align_bytes=64, name="grouped")
                 for b in range(len(row_blocks)):
-                    bank = transpose_pair(raw, 2 * b, col)
-                    regroup(nc.vector.tensor_copy if b == 0 and g % 2 == 0 else nc.scalar.copy, grouped, b * PAIR, bank)
-                staged[g] = grouped
+                    for g in run:
+                        bank = transpose_pair(raws[g // SLOT_PASSES], 2 * b, (g % SLOT_PASSES) * PASS)
+                        regroup(nc.vector.tensor_copy if b == 0 else nc.scalar.copy, staged[g], b * PAIR, bank)
 
-            def quantise_pass(g):
-                codes = packed_pool.tile([P, X_WORDS + W_WORDS], U32, align_bytes=64)
-                scales = packed_pool.tile([P, X_WORDS + W_WORDS], U8, align_bytes=64)
-                quantise(staged[g], codes, scales, 0, X_WORDS)
-                quantise(staged[g], codes, scales, X_WORDS, W_WORDS)
-                packed[g] = (codes, scales)
+            def quantise_run(run):
+                for g in run:
+                    codes = packed_pool.tile([P, X_WORDS + W_WORDS], U32, align_bytes=64)
+                    scales = packed_pool.tile([P, X_WORDS + W_WORDS], U8, align_bytes=64)
+                    packed[g] = (codes, scales)
+                for first_word, words in ((0, X_WORDS), (X_WORDS, W_WORDS)):
+                    for g in run:
+                        quantise(staged[g], packed[g][0], packed[g][1], first_word, words)
 
             def multiply_pass(g):
                 codes, scales = packed[g]
@@ -162,10 +162,10 @@ def tile_visualdeconfounder_pa_k_kernel(tc, x, Wy_w, Wy_b, k, prior, out):
                     )
 
             def stage_in_keys(part):
-                grouped = stage.tile([P, 4 * BANK], BF16, align_bytes=64)
+                grouped = stage.tile([P, 4 * BANK], BF16, align_bytes=64, name="grouped")
                 for half in range(2):
                     bank = transpose_pair(keys_raw, 4 * part + 2 * half, 0)
-                    regroup(nc.scalar.copy if part % 2 == 0 else nc.vector.tensor_copy, grouped, half * PAIR, bank)
+                    regroup(nc.scalar.copy, grouped, half * PAIR, bank)
                 key_staged[part] = grouped
 
             def quantise_keys(part):
@@ -175,26 +175,26 @@ def tile_visualdeconfounder_pa_k_kernel(tc, x, Wy_w, Wy_b, k, prior, out):
                     in_=key_staged[part][:],
                 )
 
-            for first in range(0, PASSES, RUN):
-                for g in range(first, first + RUN):
-                    stage_in(g)
-                    next_slot = g // SLOT_PASSES + RAW_BUFS
-                    if g % SLOT_PASSES == SLOT_PASSES - 1 and next_slot < SLOTS:
-                        raws[next_slot] = load_slot(next_slot)
-                        if next_slot == SLOTS - 1:
-                            load_keys_and_prior()
-                    if g >= 1:
-                        quantise_pass(g - 1)
-                for g in range(max(first - LAG, 0), first + RUN - LAG):
-                    multiply_pass(g)
+            first = 0
+            for slot in range(SLOTS):
+                for width in piece_widths(slot):
+                    run = range(first, first + width // PASS)
+                    stage_in(run)
+                    quantise_run(run)
+                    for g in run:
+                        if g >= LAG:
+                            multiply_pass(g - LAG)
+                    first += width // PASS
+                if slot + RAW_BUFS < SLOTS:
+                    raws[slot + RAW_BUFS] = load_slot(slot + RAW_BUFS)
+                    if slot + RAW_BUFS == SLOTS - 1:
+                        load_the_rest()
 
-            quantise_pass(PASSES - 1)
-            for g in range(PASSES - LAG, PASSES - 2):
-                multiply_pass(g)
             stage_in_keys(0)
             stage_in_keys(1)
-            for g in range(PASSES - 2, PASSES):
+            for g in range(PASSES - LAG, PASSES):
                 multiply_pass(g)
+            quantise_keys(0)
 
             q_planes = const.tile([P, Q_TILES, ROWS], BF16)
             for t in range(Q_TILES):
@@ -216,7 +216,7 @@ def tile_visualdeconfounder_pa_k_kernel(tc, x, Wy_w, Wy_b, k, prior, out):
             nc.vector.quantize_mx(
                 out=q_codes[:].bitcast(FP8X4), scales=q_scales[:], in_=q_grouped[:].rearrange("p c t -> p (c t)")
             )
-            for part in range(KEY_PARTS):
+            for part in range(1, KEY_PARTS):
                 quantise_keys(part)
 
         out_rows = out.rearrange("(p i) j -> p i j", i=2)

from contextlib import ExitStack

import concourse.mybir as mybir
from concourse.masks import make_identity

F32 = mybir.dt.float32
BF16 = mybir.dt.bfloat16
U32 = mybir.dt.uint32
U8 = mybir.dt.uint8
FP8X4 = mybir.dt.float8_e4m3fn_x4
ACT = mybir.ActivationFunctionType
ALU = mybir.AluOpType
AXIS = mybir.AxisListType

P = 128
PASS = 4 * P
PAIR = 2 * P
BANK = 512

ROWS, FEATURES, WIDTH, KEYS = 256, 16384, 512, 1536
PASSES = FEATURES // PASS
Q_TILES = WIDTH // P
SCALE = WIDTH ** -0.5

SLOT = 4 * PASS
SLOTS = FEATURES // SLOT
SLOT_PASSES = SLOT // PASS
RAW_BUFS = 4
LAG = 2
STAGE_BUFS = 2 * SLOT_PASSES
PACKED_BUFS = 2 * SLOT_PASSES
RING = 6
KEY_PARTS = KEYS // BANK

X_WORDS = PAIR
W_WORDS = 2 * PAIR

FLOPS = 2 * ROWS * FEATURES * WIDTH + 2 * ROWS * WIDTH * KEYS


def piece_widths(slot):
    if slot == 0:
        return (PASS, PASS, 2 * PASS)
    if slot == SLOTS - 1:
        return (2 * PASS, PASS, PASS)
    return (SLOT,)


def tile_visualdeconfounder_pa_k_kernel(tc, x, Wy_w, Wy_b, k, prior, out):
    nc = tc.nc
    row_blocks = (x, Wy_w[0:PAIR, :], Wy_w[PAIR : 2 * PAIR, :])

    with ExitStack() as ctx:
        ctx.enter_context(tc.manual_schedule())
        const = ctx.enter_context(tc.tile_pool(name="const", bufs=1))
        raw_pool = ctx.enter_context(tc.tile_pool(name="raw", bufs=RAW_BUFS))
        stage = ctx.enter_context(tc.tile_pool(name="stage", bufs=STAGE_BUFS))
        packed_pool = ctx.enter_context(tc.tile_pool(name="packed", bufs=PACKED_BUFS))
        small = ctx.enter_context(tc.tile_pool(name="small", bufs=2))

        def load_slot(slot):
            raw = raw_pool.tile([P, 2 * len(row_blocks), SLOT], BF16)
            start = 0
            for width in piece_widths(slot):
                for b, rows in enumerate(row_blocks):
                    nc.sync.dma_start(
                        out=raw[:, 2 * b : 2 * b + 2, start : start + width],
                        in_=rows[:, slot * SLOT + start : slot * SLOT + start + width].rearrange(
                            "(p i) f -> p i f", i=2
                        ),
                    )
                start += width
            return raw

        def load_the_rest():
            nc.sync.dma_start(
                out=bias_bf16[:].rearrange("p (u i) -> p u i", i=2),
                in_=Wy_b.rearrange("(u p i) -> p u i", u=2, i=2),
            )
            nc.gpsimd.tensor_copy(out=bias[:], in_=bias_bf16[:])
            for part in range(KEY_PARTS):
                nc.sync.dma_start(
                    out=keys_raw[:, 4 * part : 4 * part + 4, :],
                    in_=k[BANK * part : BANK * (part + 1), :].rearrange("(j p) e -> p j e", p=P),
                )
            nc.sync.dma_start(out=prior_all[:], in_=prior.partition_broadcast(P))

        ident = const.tile([P, P], F32)
        make_identity(nc, ident[:])
        bias_bf16 = const.tile([P, Q_TILES], BF16)
        bias = const.tile([P, Q_TILES], F32)
        warm = const.tile([P, 1], F32)
        nc.vector.memset(warm[:], 0.0)
        nc.scalar.activation(out=warm[:], in_=warm[:], func=ACT.Exp)

        raws = {}
        keys_raw = const.tile([P, KEYS // P, WIDTH], BF16)
        for slot in range(RAW_BUFS):
            raws[slot] = load_slot(slot)

        key_codes = const.tile([P, KEYS], U32, align_bytes=64)
        key_scales = const.tile([P, KEYS], U8, align_bytes=64)
        q_codes = const.tile([P, ROWS], U32, align_bytes=64)
        q_scales = const.tile([P, ROWS], U8, align_bytes=64)
        prior_all = const.tile([P, KEYS], BF16)

        with tc.psum_pool(name="acc", bufs=1) as acc_pool, tc.psum_pool(name="ring", bufs=RING) as ring:
            acc = [acc_pool.tile([P, 2, ROWS], F32, name="acc%d" % u) for u in range(Q_TILES // 2)]

            def transpose_pair(tiles, first, col):
                bank = ring.tile([P, 2, PAIR], F32)
                for i in range(2):
                    words = tiles[:, first + i, col : col + PASS].bitcast(F32)
                    for u in range(2):
                        nc.tensor.transpose(bank[:, u, i * P : (i + 1) * P], words[:, u * P : (u + 1) * P], ident[:])
                return bank

            def regroup(copy, grouped, first_word, bank):
                halves = grouped[:].bitcast(F32)[:, 2 * first_word : 2 * (first_word + PAIR)]
                copy(out=halves.rearrange("p (c u) -> p c u", u=2), in_=bank[:].rearrange("p u c -> p c u"))

            def quantise(grouped, codes, scales, first_word, words):
                nc.vector.quantize_mx(
                    out=codes[:, first_word : first_word + words].bitcast(FP8X4),
                    scales=scales[:, first_word : first_word + words],
                    in_=grouped[:, 4 * first_word : 4 * (first_word + words)],
                )

            staged = {}
            packed = {}
            key_staged = {}

            def stage_in(run):
                for g in run:
                    staged[g] = stage.tile([P, 4 * (X_WORDS + W_WORDS)], BF16, align_bytes=64, name="grouped")
                for b in range(len(row_blocks)):
                    for g in run:
                        bank = transpose_pair(raws[g // SLOT_PASSES], 2 * b, (g % SLOT_PASSES) * PASS)
                        regroup(nc.vector.tensor_copy if b == 0 else nc.scalar.copy, staged[g], b * PAIR, bank)

            def quantise_run(run):
                for g in run:
                    codes = packed_pool.tile([P, X_WORDS + W_WORDS], U32, align_bytes=64)
                    scales = packed_pool.tile([P, X_WORDS + W_WORDS], U8, align_bytes=64)
                    packed[g] = (codes, scales)
                for first_word, words in ((0, X_WORDS), (X_WORDS, W_WORDS)):
                    for g in run:
                        quantise(staged[g], packed[g][0], packed[g][1], first_word, words)

            def multiply_pass(g):
                codes, scales = packed[g]
                for t in range(Q_TILES):
                    w_cols = slice(X_WORDS + t * P, X_WORDS + (t + 1) * P)
                    nc.tensor.matmul_mx(
                        out=acc[t // 2][:, t % 2, :],
                        lhsT=codes[:, w_cols].bitcast(FP8X4),
                        lhsT_scale=scales[:, w_cols],
                        rhs=codes[:, 0:X_WORDS].bitcast(FP8X4),
                        rhs_scale=scales[:, 0:X_WORDS],
                        start=(g == 0 and t % 2 == 0),
                        stop=(g == PASSES - 1 and t % 2 == 1),
                    )

            def stage_in_keys(part):
                grouped = stage.tile([P, 4 * BANK], BF16, align_bytes=64, name="grouped")
                for half in range(2):
                    bank = transpose_pair(keys_raw, 4 * part + 2 * half, 0)
                    regroup(nc.scalar.copy, grouped, half * PAIR, bank)
                key_staged[part] = grouped

            def quantise_keys(part):
                nc.vector.quantize_mx(
                    out=key_codes[:, part * BANK : (part + 1) * BANK].bitcast(FP8X4),
                    scales=key_scales[:, part * BANK : (part + 1) * BANK],
                    in_=key_staged[part][:],
                )

            first = 0
            for slot in range(SLOTS):
                for width in piece_widths(slot):
                    run = range(first, first + width // PASS)
                    stage_in(run)
                    quantise_run(run)
                    for g in run:
                        if g >= LAG:
                            multiply_pass(g - LAG)
                    first += width // PASS
                if slot + RAW_BUFS < SLOTS:
                    raws[slot + RAW_BUFS] = load_slot(slot + RAW_BUFS)
                    if slot + RAW_BUFS == SLOTS - 1:
                        load_the_rest()

            stage_in_keys(0)
            stage_in_keys(1)
            for g in range(PASSES - LAG, PASSES):
                multiply_pass(g)
            quantise_keys(0)

            q_planes = const.tile([P, Q_TILES, ROWS], BF16)
            for t in range(Q_TILES):
                if t // 2 == 0:
                    nc.scalar.activation(
                        out=q_planes[:, t, :], in_=acc[t // 2][:, t % 2, :], func=ACT.Identity, bias=bias[:, t : t + 1]
                    )
                else:
                    nc.vector.tensor_scalar(
                        out=q_planes[:, t, :],
                        in0=acc[t // 2][:, t % 2, :],
                        scalar1=bias[:, t : t + 1],
                        scalar2=None,
                        op0=ALU.add,
                    )
            stage_in_keys(2)
            q_grouped = const.tile([P, ROWS, Q_TILES], BF16, align_bytes=64)
            nc.vector.tensor_copy(out=q_grouped[:], in_=q_planes[:].rearrange("p t c -> p c t"))
            nc.vector.quantize_mx(
                out=q_codes[:].bitcast(FP8X4), scales=q_scales[:], in_=q_grouped[:].rearrange("p c t -> p (c t)")
            )
            for part in range(1, KEY_PARTS):
                quantise_keys(part)

        out_rows = out.rearrange("(p i) j -> p i j", i=2)
        weights = const.tile([P, 2, KEYS], F32)
        with tc.psum_pool(name="scores", bufs=2 * KEY_PARTS) as score_pool:
            scores = {}
            for part in range(KEY_PARTS):
                for i in range(2):
                    score = score_pool.tile([P, BANK], F32)
                    nc.tensor.matmul_mx(
                        out=score[:],
                        lhsT=q_codes[:, i * P : (i + 1) * P].bitcast(FP8X4),
                        lhsT_scale=q_scales[:, i * P : (i + 1) * P],
                        rhs=key_codes[:, part * BANK : (part + 1) * BANK].bitcast(FP8X4),
                        rhs_scale=key_scales[:, part * BANK : (part + 1) * BANK],
                        start=True,
                        stop=True,
                    )
                    scores[i, part] = score

            sums = {}
            for i in range(2):
                part_max = small.tile([P, KEY_PARTS], F32)
                for part in range(KEY_PARTS):
                    nc.vector.tensor_reduce(out=part_max[:, part : part + 1], in_=scores[i, part][:], axis=AXIS.X, op=ALU.max)
                row_max = small.tile([P, 1], F32)
                nc.vector.tensor_reduce(out=row_max[:], in_=part_max[:], axis=AXIS.X, op=ALU.max)
                shift = small.tile([P, 1], F32)
                nc.vector.tensor_scalar(out=shift[:], in0=row_max[:], scalar1=-SCALE, scalar2=None, op0=ALU.mult)
                part_sum = small.tile([P, KEY_PARTS], F32)
                for part in range(KEY_PARTS):
                    nc.scalar.activation(
                        out=weights[:, i, part * BANK : (part + 1) * BANK],
                        in_=scores[i, part][:],
                        func=ACT.Exp,
                        bias=shift[:],
                        scale=SCALE,
                        accum_out=part_sum[:, part : part + 1],
                    )
                sums[i] = part_sum

            for i in range(2):
                row_sum = small.tile([P, 1], F32)
                nc.vector.tensor_reduce(out=row_sum[:], in_=sums[i][:], axis=AXIS.X, op=ALU.add)
                inverse = small.tile([P, 1], F32)
                nc.vector.reciprocal(out=inverse[:], in_=row_sum[:])
                for part in range(KEY_PARTS):
                    cols = slice(part * BANK, (part + 1) * BANK)
                    nc.vector.scalar_tensor_tensor(
                        out=weights[:, i, cols],
                        in0=weights[:, i, cols],
                        scalar=inverse[:],
                        in1=prior_all[:, cols],
                        op0=ALU.mult,
                        op1=ALU.mult,
                    )
                    nc.sync.dma_start(out=out_rows[:, i, cols], in_=weights[:, i, cols])
